import numpy as np
import ml_dtypes


def mxq(x, axis, fmt="e4m3"):
    dtype, down = {"e4m3": (ml_dtypes.float8_e4m3fn, 7), "e5m2": (ml_dtypes.float8_e5m2, 14)}[fmt]
    v = np.moveaxis(np.asarray(x, np.float32).astype(ml_dtypes.bfloat16).astype(np.float64), axis, -1)
    blocks = v.reshape(v.shape[:-1] + (-1, 32))
    amax = np.abs(blocks).max(-1, keepdims=True)
    byte = np.maximum(np.where(amax > 0, np.frexp(amax)[1] - 1 + 127, 0) - down, 1)
    scale = np.exp2(byte - 127.0)
    codes = (blocks / scale).astype(np.float32).astype(dtype).astype(np.float64)
    return np.moveaxis((codes * scale).reshape(v.shape), -1, axis)


WIDE = False


def mx_kscale(k):
    if not WIDE:
        return np.ones(k)
    levels = np.array([10, -10, 5, -5, 0])
    if k % 512:
        return np.exp2(np.random.permutation(np.resize(levels, k // 32))).repeat(32)
    a = np.empty((k // 512, 16))
    for p in range(k // 512):
        a[p, :8] = np.random.permutation(np.resize(levels, 8))
        for g in range(8):
            far = levels[np.abs(levels - a[p, g]) >= 10]
            a[p, g + 8] = far[np.random.randint(len(far))]
    return np.exp2(a.ravel()).repeat(32)


BF16 = ml_dtypes.bfloat16


def bf(x):
    return np.asarray(x, np.float32).astype(BF16)


def f64(x):
    return np.asarray(x).astype(np.float64)


B, K, F, INCH, OUTCH, R = 2, 4, 128, 2048, 2048, 128


def erf(a):
    c = np.clip(a, -6.0, 6.0)
    c2 = 2.0 * c * c
    t = c.copy()
    s = c.copy()
    n = 1.0
    while np.max(np.abs(t) - 1e-18 * np.abs(s)) > 0.0:
        n += 2.0
        t = t * c2 / n
        s = s + t
    return 2.0 / np.sqrt(np.pi) * np.exp(-c * c) * s


def gelu(t):
    return 0.5 * t * (1.0 + erf(t / np.sqrt(2.0)))


def setup_inputs():
    s = mx_kscale(INCH)
    return {
        "h": bf(gelu(np.random.standard_normal((B, K, F, INCH))) * s),
        "z": bf(np.random.standard_normal((B, K, F, R)) * 0.35),
        "u": bf(np.random.standard_normal((B, K, OUTCH, R)) * 1.5 * np.sqrt(R)),
        "b": bf(np.random.standard_normal((B, 1, 1, OUTCH)) * 0.3),
        "W_out": bf(np.random.standard_normal((OUTCH, INCH)) * 1.5 / np.sqrt(INCH) / s),
        "b_out": bf(np.random.standard_normal(OUTCH) * 0.3),
    }


def reference(h, z, u, b, W_out, b_out):
    lora = f64(z) @ f64(u).transpose(0, 1, 3, 2) / R
    main = mxq(f64(h), 3, "e4m3") @ mxq(f64(W_out).T, 0, "e4m3")
    return gelu(main + f64(b_out) + lora + f64(b))

@@ -1,0 +1,384 @@
+from contextlib import ExitStack
+
+import concourse.mybir as mybir
+from concourse.masks import make_identity
+
+F32 = mybir.dt.float32
+BF16 = mybir.dt.bfloat16
+U32 = mybir.dt.uint32
+U8 = mybir.dt.uint8
+I32 = mybir.dt.int32
+FP8X4 = mybir.dt.float8_e4m3fn_x4
+GELU = mybir.ActivationFunctionType.Gelu
+MULT = mybir.AluOpType.mult
+ADD = mybir.AluOpType.add
+
+P = 128
+GROUPS = 8
+CHUNKS = 4
+PASSES = 4
+NCOL = 512
+KDIM = 2048
+ODIM = 2048
+RANK = 128
+FLOPS = 2 * GROUPS * P * ODIM * (KDIM + RANK)
+
+LATE_STEP = 2
+FINE_STEPS = 3 if LATE_STEP == 2 else 2
+TAIL_CUTS = 2
+LEAD = 6
+VEC_BLK = {1: (0,), 3: (0,), 4: (0,)}
+W1_AT = ((1, 0, 0), (2, 0, 1), (3, 1, 0), (3, 1, 1), (4, 2, 0), (4, 2, 1), (5, 3, 0), (6, 3, 1))
+
+
+def build_program():
+    units_of = [[g] for g in range(GROUPS)]
+    for c in range(1, CHUNKS):
+        for g in range(0, GROUPS, LATE_STEP):
+            units_of.append([GROUPS * c + g + i for i in range(LATE_STEP)])
+    n_steps = len(units_of)
+    n_units = GROUPS * CHUNKS
+
+    def ahead(k):
+        if 0 <= k < n_steps:
+            return [n + LEAD for n in units_of[k] if n + LEAD < n_units]
+        return []
+
+    blocks_at = {}
+    for k in range(n_steps):
+        blocks_at[k] = []
+    for g in range(2, GROUPS):
+        blocks_at[g - 2] = [("h", g, 0, 0), ("h", g, 0, 1)]
+    for k, kp, j in W1_AT:
+        blocks_at[k].append(("w", 1, kp, j))
+    per = GROUPS // LATE_STEP
+    for c in (2, 3):
+        first = GROUPS + per * (c - 2) - 1
+        for i in range(2 * PASSES):
+            blocks_at[first + (i * per) // (2 * PASSES)].append(("w", c, i // 2, i % 2))
+
+    loads_at = {
+        0: [("h", 6), ("w", 1, 2, 3)],
+        1: [("h", 7), ("w", 1, 3, 4)],
+        2: [("u", 2, 0, 8)],
+        3: [("w", 2, 0, 1), ("w", 2, 1, 2)],
+        4: [("w", 2, 2, 3), ("w", 2, 3, 4)],
+        5: [("u", 3, 0, 8)],
+        7: [("w", 3, 0, 1), ("w", 3, 1, 2)],
+        8: [("w", 3, 2, 3), ("w", 3, 3, 4)],
+    }
+
+    head = []
+    for item in (("z",), ("u", 0, 0, 4), ("u", 0, 4, 8), ("h", 0), ("w", 0, 0, 1), ("w", 0, 1, 2), ("w", 0, 2, 3),
+                 ("w", 0, 3, 4), ("h", 1), ("u", 1, 0, 4), ("h", 2), ("h", 3), ("w", 1, 0, 1)):
+        head.append(("load", item))
+
+    def lora(n):
+        return [("mm", n, 0, NCOL), ("lout", n)]
+
+    head.extend([("bias", 0, True), ("bias", 1, False), ("bias", 2, True), ("bias", 3, False), ("zt",)])
+    head.extend([("bias", 4, True), ("ut", [0, 1], "tu"), ("ut", [2, 3], "tu"), ("bias", 5, False)])
+    head.extend(lora(0) + lora(1) + [("ut", [4, 5], "tu")] + lora(2) + lora(3) + [("ut", [6, 7], "tu")])
+    head.extend([("blk", ("h", 0, 0, 0), False), ("blk", ("h", 0, 0, 1), False), ("load", ("h", 4))])
+    head.extend(lora(4))
+    head.extend([("blk", ("w", 0, 0, 0), False), ("blk", ("w", 0, 0, 1), False), ("flush", 1)])
+    head.extend(lora(5))
+    head.extend([("blk", ("w", 0, 1, 0), False), ("blk", ("w", 0, 1, 1), False), ("flush", 1)])
+    head.extend(lora(6))
+    head.extend([("blk", ("w", 0, 2, 0), False), ("blk", ("w", 0, 2, 1), False), ("flush", 1)])
+    head.extend([("bias", 6, True)])
+    head.extend([("blk", ("w", 0, 3, 0), True), ("blk", ("w", 0, 3, 1), False), ("flush", 0)])
+    head.extend([("bias", 7, True)])
+    head.extend([("blk", ("h", 1, 0, 0), True), ("blk", ("h", 1, 0, 1), False)])
+    head.extend([("load", ("h", 5)), ("load", ("w", 1, 1, 2)), ("load", ("u", 1, 4, 8))])
+
+    steps = []
+    for k in range(n_steps):
+        ops = []
+        us = units_of[k]
+        vec = VEC_BLK.get(k, ())
+        blks = [("blk", blk, i in vec) for i, blk in enumerate(blocks_at[k])]
+        fine = k >= n_steps - FINE_STEPS
+        if len(us) == 1:
+            ops.append(("flush", 0))
+            ops.append(("add", us[0], 0, 0, P))
+        else:
+            for i in range(len(us)):
+                if k == n_steps - 1 and i == len(us) - 1:
+                    w = P // TAIL_CUTS
+                    for j in range(TAIL_CUTS):
+                        ops.append(("add", us[i], i, w * j, w * j + w))
+                        ops.append(("fin", i, i + 1, 4 * w * j, 4 * w * j + 4 * w))
+                else:
+                    ops.append(("add", us[i], i, 0, P))
+                    if i == 0:
+                        ops.append(("flush", 0))
+                    if fine:
+                        ops.append(("fin", i, i + 1, 0, NCOL))
+                    elif i % 2 == 1 and i < len(us) - 1:
+                        ops.append(("fin", i - 1, i + 1, 0, NCOL))
+        nxt = ahead(k + 1)
+        nxt2 = ahead(k + 2)
+        if nxt2:
+            ops.append(("utmm", nxt2, nxt))
+        else:
+            for n in nxt:
+                ops.append(("mm", n, 0, NCOL))
+        for n in nxt:
+            ops.append(("lout", n))
+        ops.extend(blks)
+        for item in loads_at.get(k, []):
+            ops.append(("load", item))
+        if not fine:
+            ops.append(("fin", len(us) - min(2, len(us)), len(us), 0, NCOL))
+        steps.append((us, ops))
+    return head, steps
+
+
+def tile_loratacmlp4_pb_kernel(tc, h, z, u, b, W_out, b_out, out):
+    nc = tc.nc
+    h_v = h.rearrange("b k f c -> (b k) f c")
+    w_v = W_out.rearrange("(c p t) k -> c p t k", p=P, t=4)
+    u_v = u.rearrange("b k (c p t) r -> c p (b k) (t r)", p=P, t=4)
+    z_v = z.rearrange("b k f r -> f (b k) r")
+    b_v = b.rearrange("b x y o -> (b x y) o")
+    bo_v = b_out.rearrange("(x o) -> x o", x=1)
+    out_v = out.rearrange("b k f o -> f (b k) o")
+
+    head, steps = build_program()
+
+    with ExitStack() as ctx:
+        const = ctx.enter_context(tc.tile_pool(name="const", bufs=1))
+        hraw_pool = ctx.enter_context(tc.tile_pool(name="hraw", bufs=4))
+        wraw_pool = ctx.enter_context(tc.tile_pool(name="wraw", bufs=8))
+        uraw_pool = ctx.enter_context(tc.tile_pool(name="uraw", bufs=3))
+        ut_pool = ctx.enter_context(tc.tile_pool(name="ut", bufs=3))
+        grp_pool = ctx.enter_context(tc.tile_pool(name="grouped", bufs=4))
+        wq_pool = ctx.enter_context(tc.tile_pool(name="wq", bufs=2))
+        l_pool = ctx.enter_context(tc.tile_pool(name="lsum", bufs=LEAD + 1 + LATE_STEP))
+        o_pool = ctx.enter_context(tc.tile_pool(name="res", bufs=(5 if LATE_STEP == 2 else 3)))
+        psum = ctx.enter_context(tc.psum_pool(name="psum", bufs=8))
+        ctx.enter_context(tc.manual_schedule())
+
+        hraw = {}
+        wraw = {}
+        uraw = {}
+        ut = {}
+        grouped = {}
+        wcodes = {}
+        wscales = {}
+        lora_ps = {}
+        lsum = {}
+        main = {}
+        pending = []
+        done = [0]
+
+        ident_f = const.tile([P, P], F32, name="ident_f")
+        ident_b = const.tile([P, P], BF16, name="ident_b")
+        rows = const.tile([P, ODIM], BF16, name="rows")
+        sel = [const.tile([P, P], BF16, name="sel%d" % i) for i in range(2)]
+        bias = const.tile([P, 2, ODIM], F32, name="bias")
+        zraw = const.tile([P, GROUPS, RANK], BF16, name="zraw")
+        z_t = const.tile([P, GROUPS, P], BF16, name="z_t")
+        hcodes = const.tile([P, GROUPS, PASSES * P], U32, name="hcodes", align_bytes=64)
+        hscales = const.tile([P, GROUPS, PASSES * P], U8, name="hscales", align_bytes=64)
+        warm = const.tile([P, 8], F32, name="warm")
+
+        def load_h(g):
+            hraw[g] = hraw_pool.tile([P, KDIM], BF16, name="hraw%d" % g, tag="hraw")
+            nc.sync.dma_start(out=hraw[g][:], in_=h_v[g])
+
+        def load_w(c, k0, k1):
+            t = wraw_pool.tile([P, 4, 512 * (k1 - k0)], BF16, name="wraw%d_%d" % (c, k0), tag="wraw")
+            nc.sync.dma_start(out=t[:], in_=w_v[c][:, :, 512 * k0:512 * k1])
+            for kp in range(k0, k1):
+                wraw[(c, kp)] = (t, kp - k0)
+
+        def load_u(c, g0, g1):
+            if c not in uraw:
+                uraw[c] = uraw_pool.tile([P, GROUPS, NCOL], BF16, name="uraw%d" % c, tag="uraw")
+            nc.sync.dma_start(out=uraw[c][:, g0:g1, :], in_=u_v[c][:, g0:g1, :])
+
+        def do_load(item):
+            if item[0] == "z":
+                nc.sync.dma_start(out=zraw[:], in_=z_v)
+            elif item[0] == "h":
+                load_h(item[1])
+            elif item[0] == "w":
+                load_w(item[1], item[2], item[3])
+            else:
+                load_u(item[1], item[2], item[3])
+
+        def copy_out(on_vector, dst, src):
+            if on_vector:
+                nc.vector.tensor_copy(out=dst, in_=src)
+            else:
+                nc.scalar.copy(out=dst, in_=src)
+
+        def block(blk, on_vector):
+            kind, a0, kp0, j = blk
+            key = (kind, a0, kp0)
+            if key not in grouped:
+                grouped[key] = grp_pool.tile([P, 4 * NCOL], BF16, name="grp_%s%d_%d" % key, tag="grp", align_bytes=64)
+            ps = psum.tile([P, 2, 2, P], F32, name="tw_%s%d_%d_%d" % blk, tag="bank")
+            for a in range(2):
+                for v in range(2):
+                    if kind == "h":
+                        w0 = 256 * (2 * j + a)
+                        src = hraw[a0][:].bitcast(F32)[:, w0 + v:w0 + 256:2]
+                    else:
+                        wt, kl = wraw[(a0, kp0)]
+                        w0 = 256 * kl
+                        src = wt[:, 2 * j + a, :].bitcast(F32)[:, w0 + v:w0 + 256:2]
+                    nc.tensor.transpose(ps[:, a, v, :], src, ident_f[:])
+            dst = grouped[key][:].bitcast(F32).rearrange("q (a r v) -> q a r v", a=4, v=2)
+            copy_out(on_vector, dst[:, 2 * j:2 * j + 2, :, :], ps[:].rearrange("q a v r -> q a r v"))
+            if j == 1:
+                pending.append(key)
+
+        def quantise(key):
+            kind, a0, kp0 = key
+            if kind == "h":
+                codes = hcodes[:, a0, :]
+                scales = hscales[:, a0, :]
+            else:
+                if a0 not in wcodes:
+                    wcodes[a0] = wq_pool.tile([P, PASSES, NCOL], U32, name="wcodes%d" % a0, tag="wcodes", align_bytes=64)
+                    wscales[a0] = wq_pool.tile([P, PASSES, NCOL], U8, name="wscales%d" % a0, tag="wscales", align_bytes=64)
+                codes = wcodes[a0][:, kp0, :]
+                scales = wscales[a0][:, kp0, :]
+            nc.vector.quantize_mx(out=codes.bitcast(FP8X4), scales=scales, in_=grouped[key][:])
+
+        def flush(keep):
+            while len(pending) - done[0] > keep:
+                quantise(pending[done[0]])
+                done[0] = done[0] + 1
+
+        def mx(n):
+            c, g = divmod(n, GROUPS)
+            main[n] = psum.tile([P, NCOL], F32, name="acc%d" % n, tag="bank")
+            for kp in range(PASSES):
+                nc.tensor.matmul_mx(
+                    out=main[n][:],
+                    lhsT=hcodes[:, g, P * kp:P * kp + P].bitcast(FP8X4),
+                    lhsT_scale=hscales[:, g, P * kp:P * kp + P],
+                    rhs=wcodes[c][:, kp, :].bitcast(FP8X4),
+                    rhs_scale=wscales[c][:, kp, :],
+                    start=(kp == 0),
+                    stop=(kp == PASSES - 1),
+                )
+
+        def by_column(ap):
+            return ap.rearrange("q (p t) -> q p t", t=4)
+
+        def by_plane(ap):
+            return ap.rearrange("q (t p) -> q p t", t=4)
+
+        def add_main(n, dst, p0, p1):
+            nc.vector.tensor_tensor(out=by_column(dst)[:, p0:p1, :], in0=by_plane(main[n][:])[:, p0:p1, :],
+                                    in1=by_column(lsum[n][:])[:, p0:p1, :], op=ADD)
+
+        def u_transposes(us, tag):
+            tu = psum.tile([P, len(us), 4, P], BF16, name="tu%d" % us[0], tag="bank")
+            for i in range(len(us)):
+                c, g = divmod(us[i], GROUPS)
+                for t in range(4):
+                    nc.tensor.transpose(tu[:, i, t, :], uraw[c][:, g, P * t:P * t + P], ident_b[:])
+            t_sb = ut_pool.tile([P, len(us), NCOL], BF16, name="ut%d" % us[0], tag="ut")
+            nc.scalar.copy(out=t_sb[:], in_=tu[:].rearrange("q i t p -> q i (t p)"))
+            for i in range(len(us)):
+                ut[us[i]] = t_sb[:, i, :]
+
+        def u_woven(us, mms):
+            tu = psum.tile([P, len(us), 4, P], BF16, name="tu%d" % us[0], tag="bank")
+            for i in range(max(len(us), len(mms))):
+                if i < len(mms):
+                    lora_mm(mms[i], 0, NCOL)
+                if i < len(us):
+                    c, g = divmod(us[i], GROUPS)
+                    for t in range(4):
+                        nc.tensor.transpose(tu[:, i, t, :], uraw[c][:, g, P * t:P * t + P], ident_b[:])
+            t_sb = ut_pool.tile([P, len(us), NCOL], BF16, name="ut%d" % us[0], tag="ut")
+            nc.scalar.copy(out=t_sb[:], in_=tu[:].rearrange("q i t p -> q i (t p)"))
+            for i in range(len(us)):
+                ut[us[i]] = t_sb[:, i, :]
+
+        def lora_mm(n, c0, c1):
+            g = n % GROUPS
+            if c0 == 0:
+                lora_ps[n] = psum.tile([P, NCOL], F32, name="lo%d" % n, tag="bank")
+            nc.tensor.matmul(out=lora_ps[n][:, c0:c1], lhsT=z_t[:, g, :], rhs=ut[n][:, c0:c1], start=True, stop=True)
+
+        def lora_out(n):
+            c, g = divmod(n, GROUPS)
+            lsum[n] = l_pool.tile([P, NCOL], F32, name="lsum%d" % n, tag="lsum")
+            nc.vector.scalar_tensor_tensor(
+                out=by_column(lsum[n][:]),
+                in0=by_plane(lora_ps[n][:]),
+                scalar=1.0 / RANK,
+                in1=by_column(bias[:, g // 4, NCOL * c:NCOL * c + NCOL]),
+                op0=MULT,
+                op1=ADD,
+            )
+
+        def finish(res, us, i0, i1, c0, c1):
+            c, g = divmod(us[i0], GROUPS)
+            nc.scalar.activation(out=res[:, i0:i1, c0:c1], in_=res[:, i0:i1, c0:c1], func=GELU)
+            nc.sync.dma_start(out=out_v[:, g:g + i1 - i0, NCOL * c + c0:NCOL * c + c1], in_=res[:, i0:i1, c0:c1])
+
+        def bias_mm(i, on_vector):
+            c, bb = divmod(i, 2)
+            ps = psum.tile([P, NCOL], F32, name="bias_ps%d" % i, tag="bank")
+            nc.tensor.matmul(out=ps[:], lhsT=sel[bb][:], rhs=rows[:, NCOL * c:NCOL * c + NCOL], start=True, stop=True)
+            copy_out(on_vector, bias[:, bb, NCOL * c:NCOL * c + NCOL], ps[:])
+
+        def z_transposes():
+            tz = psum.tile([P, GROUPS, P], BF16, name="tz", tag="bank")
+            for g in range(GROUPS):
+                nc.tensor.transpose(tz[:, g, :], zraw[:, g, :], ident_b[:])
+            nc.scalar.copy(out=z_t[:], in_=tz[:])
+
+        def run(ops, us, res):
+            for op in ops:
+                if op[0] == "add":
+                    add_main(op[1], res[:, op[2], :], op[3], op[4])
+                elif op[0] == "mm":
+                    lora_mm(op[1], op[2], op[3])
+                elif op[0] == "bias":
+                    bias_mm(op[1], op[2])
+                elif op[0] == "flush":
+                    flush(op[1])
+                elif op[0] == "lout":
+                    lora_out(op[1])
+                elif op[0] == "ut":
+                    u_transposes(op[1], op[2])
+                elif op[0] == "utmm":
+                    u_woven(op[1], op[2])
+                elif op[0] == "zt":
+                    z_transposes()
+                elif op[0] == "blk":
+                    block(op[1], op[2])
+                elif op[0] == "load":
+                    do_load(op[1])
+                else:
+                    finish(res, us, op[1], op[2], op[3], op[4])
+
+        nc.vector.memset(rows[:].bitcast(I32), 0)
+        nc.sync.dma_start(out=rows[0:1, :], in_=bo_v)
+        nc.sync.dma_start(out=rows[32:33, :], in_=b_v[0:1, :])
+        nc.sync.dma_start(out=rows[64:65, :], in_=b_v[1:2, :])
+        make_identity(nc, ident_b[:])
+        make_identity(nc, ident_f[:])
+        for i in range(2):
+            nc.vector.memset(sel[i][:], 0.0)
+            nc.vector.memset(sel[i][0:1, :], 1.0)
+            nc.vector.memset(sel[i][32 * (i + 1):32 * (i + 1) + 1, :], 1.0)
+        nc.vector.memset(warm[:], 0.0)
+        nc.scalar.activation(out=warm[:], in_=warm[:], func=GELU)
+        run(head, [], None)
+        for us, ops in steps:
+            res = o_pool.tile([P, len(us), NCOL], F32, name="res%d" % us[0], tag="res%d" % len(us),
+                              bufs=(5 if len(us) < 4 else 3))
+            for n in us:
+                mx(n)
+            run(ops, us, res)

@@ -23,7 +23,7 @@ ODIM = 2048
 RANK = 128
 FLOPS = 2 * GROUPS * P * ODIM * (KDIM + RANK)
 
-LATE_STEP = 2
+LATE_STEP = 4
 FINE_STEPS = 3 if LATE_STEP == 2 else 2
 TAIL_CUTS = 2
 LEAD = 6
@@ -69,19 +69,20 @@ def build_program():
     }
 
     head = []
-    for item in (("z",), ("u", 0, 0, 4), ("u", 0, 4, 8), ("h", 0), ("w", 0, 0, 1), ("w", 0, 1, 2), ("w", 0, 2, 3),
+    for item in (("z",), ("u", 0, 0, 4), ("rows",), ("u", 0, 4, 8), ("h", 0), ("w", 0, 0, 1), ("w", 0, 1, 2), ("w", 0, 2, 3),
                  ("w", 0, 3, 4), ("h", 1), ("u", 1, 0, 4), ("h", 2), ("h", 3), ("w", 1, 0, 1)):
         head.append(("load", item))
 
     def lora(n):
         return [("mm", n, 0, NCOL), ("lout", n)]
 
-    head.extend([("bias", 0, True), ("bias", 1, False), ("bias", 2, True), ("bias", 3, False), ("zt",)])
-    head.extend([("bias", 4, True), ("ut", [0, 1], "tu"), ("ut", [2, 3], "tu"), ("bias", 5, False)])
-    head.extend(lora(0) + lora(1) + [("ut", [4, 5], "tu")] + lora(2) + lora(3) + [("ut", [6, 7], "tu")])
+    head.extend([("zt",), ("ut", [0, 1], "tu"), ("bias", 0, True), ("bias", 1, False), ("ut", [2, 3], "tu")])
+    head.extend(lora(0) + [("bias", 2, True)] + lora(1) + [("ut", [4, 5], "tu")])
+    head.extend(lora(2) + [("bias", 3, False)] + lora(3) + [("ut", [6, 7], "tu"), ("bias", 4, True)])
     head.extend([("blk", ("h", 0, 0, 0), False), ("blk", ("h", 0, 0, 1), False), ("load", ("h", 4))])
     head.extend(lora(4))
     head.extend([("blk", ("w", 0, 0, 0), False), ("blk", ("w", 0, 0, 1), False), ("flush", 1)])
+    head.extend([("bias", 5, False)])
     head.extend(lora(5))
     head.extend([("blk", ("w", 0, 1, 0), False), ("blk", ("w", 0, 1, 1), False), ("flush", 1)])
     head.extend(lora(6))
@@ -119,13 +120,14 @@ def build_program():
                         ops.append(("fin", i - 1, i + 1, 0, NCOL))
         nxt = ahead(k + 1)
         nxt2 = ahead(k + 2)
-        if nxt2:
-            ops.append(("utmm", nxt2, nxt))
-        else:
-            for n in nxt:
-                ops.append(("mm", n, 0, NCOL))
-        for n in nxt:
-            ops.append(("lout", n))
+        for i in range(0, max(len(nxt), len(nxt2)), 2):
+            if nxt2[i:i + 2]:
+                ops.append(("utmm", nxt2[i:i + 2], nxt[i:i + 2]))
+            else:
+                for n in nxt[i:i + 2]:
+                    ops.append(("mm", n, 0, NCOL))
+            for n in nxt[i:i + 2]:
+                ops.append(("lout", n))
         ops.extend(blks)
         for item in loads_at.get(k, []):
             ops.append(("load", item))
@@ -152,7 +154,7 @@ def tile_loratacmlp4_pb_kernel(tc, h, z, u, b, W_out, b_out, out):
         hraw_pool = ctx.enter_context(tc.tile_pool(name="hraw", bufs=4))
         wraw_pool = ctx.enter_context(tc.tile_pool(name="wraw", bufs=8))
         uraw_pool = ctx.enter_context(tc.tile_pool(name="uraw", bufs=3))
-        ut_pool = ctx.enter_context(tc.tile_pool(name="ut", bufs=3))
+        ut_pool = ctx.enter_context(tc.tile_pool(name="ut", bufs=4))
         grp_pool = ctx.enter_context(tc.tile_pool(name="grouped", bufs=4))
         wq_pool = ctx.enter_context(tc.tile_pool(name="wq", bufs=2))
         l_pool = ctx.enter_context(tc.tile_pool(name="lsum", bufs=LEAD + 1 + LATE_STEP))
@@ -200,7 +202,11 @@ def tile_loratacmlp4_pb_kernel(tc, h, z, u, b, W_out, b_out, out):
             nc.sync.dma_start(out=uraw[c][:, g0:g1, :], in_=u_v[c][:, g0:g1, :])
 
         def do_load(item):
-            if item[0] == "z":
+            if item[0] == "rows":
+                nc.sync.dma_start(out=rows[0:1, :], in_=bo_v)
+                nc.sync.dma_start(out=rows[32:33, :], in_=b_v[0:1, :])
+                nc.sync.dma_start(out=rows[64:65, :], in_=b_v[1:2, :])
+            elif item[0] == "z":
                 nc.sync.dma_start(out=zraw[:], in_=z_v)
             elif item[0] == "h":
                 load_h(item[1])
@@ -364,9 +370,6 @@ def tile_loratacmlp4_pb_kernel(tc, h, z, u, b, W_out, b_out, out):
                     finish(res, us, op[1], op[2], op[3], op[4])
 
         nc.vector.memset(rows[:].bitcast(I32), 0)
-        nc.sync.dma_start(out=rows[0:1, :], in_=bo_v)
-        nc.sync.dma_start(out=rows[32:33, :], in_=b_v[0:1, :])
-        nc.sync.dma_start(out=rows[64:65, :], in_=b_v[1:2, :])
         make_identity(nc, ident_b[:])
         make_identity(nc, ident_f[:])
         for i in range(2):

@@ -57,6 +57,14 @@ def build_program():
         for i in range(2 * PASSES):
             blocks_at[first + (i * per) // (2 * PASSES)].append(("w", c, i // 2, i % 2))
 
+    permute_at = {}
+    seen = set()
+    for k in range(n_steps):
+        for blk in blocks_at[k]:
+            if blk[0] == "w" and blk[1] in (2, 3,) and blk[:3] not in seen:
+                seen.add(blk[:3])
+                permute_at.setdefault(k - 1, []).append(blk[:3])
+
     loads_at = {
         0: [("h", 6), ("w", 1, 2, 3)],
         1: [("h", 7), ("w", 1, 3, 4)],
@@ -128,6 +136,8 @@ def build_program():
                     ops.append(("mm", n, 0, NCOL))
             for n in nxt[i:i + 2]:
                 ops.append(("lout", n))
+        for key in permute_at.get(k, []):
+            ops.append(("permute", key))
         ops.extend(blks)
         for item in loads_at.get(k, []):
             ops.append(("load", item))
@@ -155,6 +165,7 @@ def tile_loratacmlp4_pb_kernel(tc, h, z, u, b, W_out, b_out, out):
         wraw_pool = ctx.enter_context(tc.tile_pool(name="wraw", bufs=8))
         uraw_pool = ctx.enter_context(tc.tile_pool(name="uraw", bufs=3))
         ut_pool = ctx.enter_context(tc.tile_pool(name="ut", bufs=4))
+        perm_pool = ctx.enter_context(tc.tile_pool(name="permuted", bufs=4))
         grp_pool = ctx.enter_context(tc.tile_pool(name="grouped", bufs=4))
         wq_pool = ctx.enter_context(tc.tile_pool(name="wq", bufs=2))
         l_pool = ctx.enter_context(tc.tile_pool(name="lsum", bufs=LEAD + 1 + LATE_STEP))
@@ -167,6 +178,7 @@ def tile_loratacmlp4_pb_kernel(tc, h, z, u, b, W_out, b_out, out):
         uraw = {}
         ut = {}
         grouped = {}
+        permuted = {}
         wcodes = {}
         wscales = {}
         lora_ps = {}
@@ -221,6 +233,14 @@ def tile_loratacmlp4_pb_kernel(tc, h, z, u, b, W_out, b_out, out):
             else:
                 nc.scalar.copy(out=dst, in_=src)
 
+        def permute(key):
+            kind, a0, kp0 = key
+            permuted[key] = perm_pool.tile([P, KDIM], BF16, name="perm_%s%d_%d" % key, tag="perm")
+            dst = permuted[key][:].bitcast(F32).rearrange("q (v w) -> q v w", v=2)
+            wt, kl = wraw[(a0, kp0)]
+            src = wt[:].rearrange("q t k -> q (t k)").bitcast(F32).rearrange("q (w v) -> q v w", v=2)
+            nc.vector.tensor_copy(out=dst, in_=src)
+
         def block(blk, on_vector):
             kind, a0, kp0, j = blk
             key = (kind, a0, kp0)
@@ -229,7 +249,10 @@ def tile_loratacmlp4_pb_kernel(tc, h, z, u, b, W_out, b_out, out):
             ps = psum.tile([P, 2, 2, P], F32, name="tw_%s%d_%d_%d" % blk, tag="bank")
             for a in range(2):
                 for v in range(2):
-                    if kind == "h":
+                    if key in permuted:
+                        w0 = 512 * v + 128 * (2 * j + a)
+                        src = permuted[key][:].bitcast(F32)[:, w0:w0 + 128]
+                    elif kind == "h":
                         w0 = 256 * (2 * j + a)
                         src = hraw[a0][:].bitcast(F32)[:, w0 + v:w0 + 256:2]
                     else:
@@ -362,6 +385,8 @@ def tile_loratacmlp4_pb_kernel(tc, h, z, u, b, W_out, b_out, out):
                     u_woven(op[1], op[2])
                 elif op[0] == "zt":
                     z_transposes()
+                elif op[0] == "permute":
+                    permute(op[1])
                 elif op[0] == "blk":
                     block(op[1], op[2])
                 elif op[0] == "load":

from contextlib import ExitStack

import concourse.mybir as mybir
from concourse.masks import make_identity

F32 = mybir.dt.float32
BF16 = mybir.dt.bfloat16
U32 = mybir.dt.uint32
U8 = mybir.dt.uint8
I32 = mybir.dt.int32
FP8X4 = mybir.dt.float8_e4m3fn_x4
GELU = mybir.ActivationFunctionType.Gelu
MULT = mybir.AluOpType.mult
ADD = mybir.AluOpType.add

P = 128
GROUPS = 8
CHUNKS = 4
PASSES = 4
NCOL = 512
KDIM = 2048
ODIM = 2048
RANK = 128
FLOPS = 2 * GROUPS * P * ODIM * (KDIM + RANK)

LATE_STEP = 4
FINE_STEPS = 3 if LATE_STEP == 2 else 2
TAIL_CUTS = 2
LEAD = 6
VEC_BLK = {1: (0,), 3: (0,), 4: (0,)}
W1_AT = ((1, 0, 0), (2, 0, 1), (3, 1, 0), (3, 1, 1), (4, 2, 0), (4, 2, 1), (5, 3, 0), (6, 3, 1))


def build_program():
    units_of = [[g] for g in range(GROUPS)]
    for c in range(1, CHUNKS):
        for g in range(0, GROUPS, LATE_STEP):
            units_of.append([GROUPS * c + g + i for i in range(LATE_STEP)])
    n_steps = len(units_of)
    n_units = GROUPS * CHUNKS

    def ahead(k):
        if 0 <= k < n_steps:
            return [n + LEAD for n in units_of[k] if n + LEAD < n_units]
        return []

    blocks_at = {}
    for k in range(n_steps):
        blocks_at[k] = []
    for g in range(2, GROUPS):
        blocks_at[g - 2] = [("h", g, 0, 0), ("h", g, 0, 1)]
    for k, kp, j in W1_AT:
        blocks_at[k].append(("w", 1, kp, j))
    per = GROUPS // LATE_STEP
    for c in (2, 3):
        first = GROUPS + per * (c - 2) - 1
        for i in range(2 * PASSES):
            blocks_at[first + (i * per) // (2 * PASSES)].append(("w", c, i // 2, i % 2))

    permute_at = {}
    seen = set()
    for k in range(n_steps):
        for blk in blocks_at[k]:
            if blk[0] == "w" and blk[1] in (2, 3,) and blk[:3] not in seen:
                seen.add(blk[:3])
                permute_at.setdefault(k - 1, []).append(blk[:3])

    loads_at = {
        0: [("h", 6), ("w", 1, 2, 3)],
        1: [("h", 7), ("w", 1, 3, 4)],
        2: [("u", 2, 0, 8)],
        3: [("w", 2, 0, 1), ("w", 2, 1, 2)],
        4: [("w", 2, 2, 3), ("w", 2, 3, 4)],
        5: [("u", 3, 0, 8)],
        7: [("w", 3, 0, 1), ("w", 3, 1, 2)],
        8: [("w", 3, 2, 3), ("w", 3, 3, 4)],
    }

    head = []
    for item in (("z",), ("u", 0, 0, 4), ("rows",), ("u", 0, 4, 8), ("h", 0), ("w", 0, 0, 1), ("w", 0, 1, 2), ("w", 0, 2, 3),
                 ("w", 0, 3, 4), ("h", 1), ("u", 1, 0, 4), ("h", 2), ("h", 3), ("w", 1, 0, 1)):
        head.append(("load", item))

    def lora(n):
        return [("mm", n, 0, NCOL), ("lout", n)]

    head.extend([("zt",), ("ut", [0, 1], "tu"), ("bias", 0, True), ("bias", 1, False), ("ut", [2, 3], "tu")])
    head.extend(lora(0) + [("bias", 2, True)] + lora(1) + [("ut", [4, 5], "tu")])
    head.extend(lora(2) + [("bias", 3, False)] + lora(3) + [("ut", [6, 7], "tu"), ("bias", 4, True)])
    head.extend([("blk", ("h", 0, 0, 0), False), ("blk", ("h", 0, 0, 1), False), ("load", ("h", 4))])
    head.extend(lora(4))
    head.extend([("blk", ("w", 0, 0, 0), False), ("blk", ("w", 0, 0, 1), False), ("flush", 1)])
    head.extend([("bias", 5, False)])
    head.extend(lora(5))
    head.extend([("blk", ("w", 0, 1, 0), False), ("blk", ("w", 0, 1, 1), False), ("flush", 1)])
    head.extend(lora(6))
    head.extend([("blk", ("w", 0, 2, 0), False), ("blk", ("w", 0, 2, 1), False), ("flush", 1)])
    head.extend([("bias", 6, True)])
    head.extend([("blk", ("w", 0, 3, 0), True), ("blk", ("w", 0, 3, 1), False), ("flush", 0)])
    head.extend([("bias", 7, True)])
    head.extend([("blk", ("h", 1, 0, 0), True), ("blk", ("h", 1, 0, 1), False)])
    head.extend([("load", ("h", 5)), ("load", ("w", 1, 1, 2)), ("load", ("u", 1, 4, 8))])

    steps = []
    for k in range(n_steps):
        ops = []
        us = units_of[k]
        vec = VEC_BLK.get(k, ())
        blks = [("blk", blk, i in vec) for i, blk in enumerate(blocks_at[k])]
        fine = k >= n_steps - FINE_STEPS
        if len(us) == 1:
            ops.append(("flush", 0))
            ops.append(("add", us[0], 0, 0, P))
        else:
            for i in range(len(us)):
                if k == n_steps - 1 and i == len(us) - 1:
                    w = P // TAIL_CUTS
                    for j in range(TAIL_CUTS):
                        ops.append(("add", us[i], i, w * j, w * j + w))
                        ops.append(("fin", i, i + 1, 4 * w * j, 4 * w * j + 4 * w))
                else:
                    ops.append(("add", us[i], i, 0, P))
                    if i == 0:
                        ops.append(("flush", 0))
                    if fine:
                        ops.append(("fin", i, i + 1, 0, NCOL))
                    elif i % 2 == 1 and i < len(us) - 1:
                        ops.append(("fin", i - 1, i + 1, 0, NCOL))
        nxt = ahead(k + 1)
        nxt2 = ahead(k + 2)
        for i in range(0, max(len(nxt), len(nxt2)), 2):
            if nxt2[i:i + 2]:
                ops.append(("utmm", nxt2[i:i + 2], nxt[i:i + 2]))
            else:
                for n in nxt[i:i + 2]:
                    ops.append(("mm", n, 0, NCOL))
            for n in nxt[i:i + 2]:
                ops.append(("lout", n))
        for key in permute_at.get(k, []):
            ops.append(("permute", key))
        ops.extend(blks)
        for item in loads_at.get(k, []):
            ops.append(("load", item))
        if not fine:
            ops.append(("fin", len(us) - min(2, len(us)), len(us), 0, NCOL))
        steps.append((us, ops))
    return head, steps


def tile_loratacmlp4_pb_kernel(tc, h, z, u, b, W_out, b_out, out):
    nc = tc.nc
    h_v = h.rearrange("b k f c -> (b k) f c")
    w_v = W_out.rearrange("(c p t) k -> c p t k", p=P, t=4)
    u_v = u.rearrange("b k (c p t) r -> c p (b k) (t r)", p=P, t=4)
    z_v = z.rearrange("b k f r -> f (b k) r")
    b_v = b.rearrange("b x y o -> (b x y) o")
    bo_v = b_out.rearrange("(x o) -> x o", x=1)
    out_v = out.rearrange("b k f o -> f (b k) o")

    head, steps = build_program()

    with ExitStack() as ctx:
        const = ctx.enter_context(tc.tile_pool(name="const", bufs=1))
        hraw_pool = ctx.enter_context(tc.tile_pool(name="hraw", bufs=4))
        wraw_pool = ctx.enter_context(tc.tile_pool(name="wraw", bufs=8))
        uraw_pool = ctx.enter_context(tc.tile_pool(name="uraw", bufs=3))
        ut_pool = ctx.enter_context(tc.tile_pool(name="ut", bufs=4))
        perm_pool = ctx.enter_context(tc.tile_pool(name="permuted", bufs=4))
        grp_pool = ctx.enter_context(tc.tile_pool(name="grouped", bufs=4))
        wq_pool = ctx.enter_context(tc.tile_pool(name="wq", bufs=2))
        l_pool = ctx.enter_context(tc.tile_pool(name="lsum", bufs=LEAD + 1 + LATE_STEP))
        o_pool = ctx.enter_context(tc.tile_pool(name="res", bufs=(5 if LATE_STEP == 2 else 3)))
        psum = ctx.enter_context(tc.psum_pool(name="psum", bufs=8))
        ctx.enter_context(tc.manual_schedule())

        hraw = {}
        wraw = {}
        uraw = {}
        ut = {}
        grouped = {}
        permuted = {}
        wcodes = {}
        wscales = {}
        lora_ps = {}
        lsum = {}
        main = {}
        pending = []
        done = [0]

        ident_f = const.tile([P, P], F32, name="ident_f")
        ident_b = const.tile([P, P], BF16, name="ident_b")
        rows = const.tile([P, ODIM], BF16, name="rows")
        sel = [const.tile([P, P], BF16, name="sel%d" % i) for i in range(2)]
        bias = const.tile([P, 2, ODIM], F32, name="bias")
        zraw = const.tile([P, GROUPS, RANK], BF16, name="zraw")
        z_t = const.tile([P, GROUPS, P], BF16, name="z_t")
        hcodes = const.tile([P, GROUPS, PASSES * P], U32, name="hcodes", align_bytes=64)
        hscales = const.tile([P, GROUPS, PASSES * P], U8, name="hscales", align_bytes=64)
        warm = const.tile([P, 8], F32, name="warm")

        def load_h(g):
            hraw[g] = hraw_pool.tile([P, KDIM], BF16, name="hraw%d" % g, tag="hraw")
            nc.sync.dma_start(out=hraw[g][:], in_=h_v[g])

        def load_w(c, k0, k1):
            t = wraw_pool.tile([P, 4, 512 * (k1 - k0)], BF16, name="wraw%d_%d" % (c, k0), tag="wraw")
            nc.sync.dma_start(out=t[:], in_=w_v[c][:, :, 512 * k0:512 * k1])
            for kp in range(k0, k1):
                wraw[(c, kp)] = (t, kp - k0)

        def load_u(c, g0, g1):
            if c not in uraw:
                uraw[c] = uraw_pool.tile([P, GROUPS, NCOL], BF16, name="uraw%d" % c, tag="uraw")
            nc.sync.dma_start(out=uraw[c][:, g0:g1, :], in_=u_v[c][:, g0:g1, :])

        def do_load(item):
            if item[0] == "rows":
                nc.sync.dma_start(out=rows[0:1, :], in_=bo_v)
                nc.sync.dma_start(out=rows[32:33, :], in_=b_v[0:1, :])
                nc.sync.dma_start(out=rows[64:65, :], in_=b_v[1:2, :])
            elif item[0] == "z":
                nc.sync.dma_start(out=zraw[:], in_=z_v)
            elif item[0] == "h":
                load_h(item[1])
            elif item[0] == "w":
                load_w(item[1], item[2], item[3])
            else:
                load_u(item[1], item[2], item[3])

        def copy_out(on_vector, dst, src):
            if on_vector:
                nc.vector.tensor_copy(out=dst, in_=src)
            else:
                nc.scalar.copy(out=dst, in_=src)

        def permute(key):
            kind, a0, kp0 = key
            permuted[key] = perm_pool.tile([P, KDIM], BF16, name="perm_%s%d_%d" % key, tag="perm")
            dst = permuted[key][:].bitcast(F32).rearrange("q (v w) -> q v w", v=2)
            wt, kl = wraw[(a0, kp0)]
            src = wt[:].rearrange("q t k -> q (t k)").bitcast(F32).rearrange("q (w v) -> q v w", v=2)
            nc.vector.tensor_copy(out=dst, in_=src)

        def block(blk, on_vector):
            kind, a0, kp0, j = blk
            key = (kind, a0, kp0)
            if key not in grouped:
                grouped[key] = grp_pool.tile([P, 4 * NCOL], BF16, name="grp_%s%d_%d" % key, tag="grp", align_bytes=64)
            ps = psum.tile([P, 2, 2, P], F32, name="tw_%s%d_%d_%d" % blk, tag="bank")
            for a in range(2):
                for v in range(2):
                    if key in permuted:
                        w0 = 512 * v + 128 * (2 * j + a)
                        src = permuted[key][:].bitcast(F32)[:, w0:w0 + 128]
                    elif kind == "h":
                        w0 = 256 * (2 * j + a)
                        src = hraw[a0][:].bitcast(F32)[:, w0 + v:w0 + 256:2]
                    else:
                        wt, kl = wraw[(a0, kp0)]
                        w0 = 256 * kl
                        src = wt[:, 2 * j + a, :].bitcast(F32)[:, w0 + v:w0 + 256:2]
                    nc.tensor.transpose(ps[:, a, v, :], src, ident_f[:])
            dst = grouped[key][:].bitcast(F32).rearrange("q (a r v) -> q a r v", a=4, v=2)
            copy_out(on_vector, dst[:, 2 * j:2 * j + 2, :, :], ps[:].rearrange("q a v r -> q a r v"))
            if j == 1:
                pending.append(key)

        def quantise(key):
            kind, a0, kp0 = key
            if kind == "h":
                codes = hcodes[:, a0, :]
                scales = hscales[:, a0, :]
            else:
                if a0 not in wcodes:
                    wcodes[a0] = wq_pool.tile([P, PASSES, NCOL], U32, name="wcodes%d" % a0, tag="wcodes", align_bytes=64)
                    wscales[a0] = wq_pool.tile([P, PASSES, NCOL], U8, name="wscales%d" % a0, tag="wscales", align_bytes=64)
                codes = wcodes[a0][:, kp0, :]
                scales = wscales[a0][:, kp0, :]
            nc.vector.quantize_mx(out=codes.bitcast(FP8X4), scales=scales, in_=grouped[key][:])

        def flush(keep):
            while len(pending) - done[0] > keep:
                quantise(pending[done[0]])
                done[0] = done[0] + 1

        def mx(n):
            c, g = divmod(n, GROUPS)
            main[n] = psum.tile([P, NCOL], F32, name="acc%d" % n, tag="bank")
            for kp in range(PASSES):
                nc.tensor.matmul_mx(
                    out=main[n][:],
                    lhsT=hcodes[:, g, P * kp:P * kp + P].bitcast(FP8X4),
                    lhsT_scale=hscales[:, g, P * kp:P * kp + P],
                    rhs=wcodes[c][:, kp, :].bitcast(FP8X4),
                    rhs_scale=wscales[c][:, kp, :],
                    start=(kp == 0),
                    stop=(kp == PASSES - 1),
                )

        def by_column(ap):
            return ap.rearrange("q (p t) -> q p t", t=4)

        def by_plane(ap):
            return ap.rearrange("q (t p) -> q p t", t=4)

        def add_main(n, dst, p0, p1):
            nc.vector.tensor_tensor(out=by_column(dst)[:, p0:p1, :], in0=by_plane(main[n][:])[:, p0:p1, :],
                                    in1=by_column(lsum[n][:])[:, p0:p1, :], op=ADD)

        def u_transposes(us, tag):
            tu = psum.tile([P, len(us), 4, P], BF16, name="tu%d" % us[0], tag="bank")
            for i in range(len(us)):
                c, g = divmod(us[i], GROUPS)
                for t in range(4):
                    nc.tensor.transpose(tu[:, i, t, :], uraw[c][:, g, P * t:P * t + P], ident_b[:])
            t_sb = ut_pool.tile([P, len(us), NCOL], BF16, name="ut%d" % us[0], tag="ut")
            nc.scalar.copy(out=t_sb[:], in_=tu[:].rearrange("q i t p -> q i (t p)"))
            for i in range(len(us)):
                ut[us[i]] = t_sb[:, i, :]

        def u_woven(us, mms):
            tu = psum.tile([P, len(us), 4, P], BF16, name="tu%d" % us[0], tag="bank")
            for i in range(max(len(us), len(mms))):
                if i < len(mms):
                    lora_mm(mms[i], 0, NCOL)
                if i < len(us):
                    c, g = divmod(us[i], GROUPS)
                    for t in range(4):
                        nc.tensor.transpose(tu[:, i, t, :], uraw[c][:, g, P * t:P * t + P], ident_b[:])
            t_sb = ut_pool.tile([P, len(us), NCOL], BF16, name="ut%d" % us[0], tag="ut")
            nc.scalar.copy(out=t_sb[:], in_=tu[:].rearrange("q i t p -> q i (t p)"))
            for i in range(len(us)):
                ut[us[i]] = t_sb[:, i, :]

        def lora_mm(n, c0, c1):
            g = n % GROUPS
            if c0 == 0:
                lora_ps[n] = psum.tile([P, NCOL], F32, name="lo%d" % n, tag="bank")
            nc.tensor.matmul(out=lora_ps[n][:, c0:c1], lhsT=z_t[:, g, :], rhs=ut[n][:, c0:c1], start=True, stop=True)

        def lora_out(n):
            c, g = divmod(n, GROUPS)
            lsum[n] = l_pool.tile([P, NCOL], F32, name="lsum%d" % n, tag="lsum")
            nc.vector.scalar_tensor_tensor(
                out=by_column(lsum[n][:]),
                in0=by_plane(lora_ps[n][:]),
                scalar=1.0 / RANK,
                in1=by_column(bias[:, g // 4, NCOL * c:NCOL * c + NCOL]),
                op0=MULT,
                op1=ADD,
            )

        def finish(res, us, i0, i1, c0, c1):
            c, g = divmod(us[i0], GROUPS)
            nc.scalar.activation(out=res[:, i0:i1, c0:c1], in_=res[:, i0:i1, c0:c1], func=GELU)
            nc.sync.dma_start(out=out_v[:, g:g + i1 - i0, NCOL * c + c0:NCOL * c + c1], in_=res[:, i0:i1, c0:c1])

        def bias_mm(i, on_vector):
            c, bb = divmod(i, 2)
            ps = psum.tile([P, NCOL], F32, name="bias_ps%d" % i, tag="bank")
            nc.tensor.matmul(out=ps[:], lhsT=sel[bb][:], rhs=rows[:, NCOL * c:NCOL * c + NCOL], start=True, stop=True)
            copy_out(on_vector, bias[:, bb, NCOL * c:NCOL * c + NCOL], ps[:])

        def z_transposes():
            tz = psum.tile([P, GROUPS, P], BF16, name="tz", tag="bank")
            for g in range(GROUPS):
                nc.tensor.transpose(tz[:, g, :], zraw[:, g, :], ident_b[:])
            nc.scalar.copy(out=z_t[:], in_=tz[:])

        def run(ops, us, res):
            for op in ops:
                if op[0] == "add":
                    add_main(op[1], res[:, op[2], :], op[3], op[4])
                elif op[0] == "mm":
                    lora_mm(op[1], op[2], op[3])
                elif op[0] == "bias":
                    bias_mm(op[1], op[2])
                elif op[0] == "flush":
                    flush(op[1])
                elif op[0] == "lout":
                    lora_out(op[1])
                elif op[0] == "ut":
                    u_transposes(op[1], op[2])
                elif op[0] == "utmm":
                    u_woven(op[1], op[2])
                elif op[0] == "zt":
                    z_transposes()
                elif op[0] == "permute":
                    permute(op[1])
                elif op[0] == "blk":
                    block(op[1], op[2])
                elif op[0] == "load":
                    do_load(op[1])
                else:
                    finish(res, us, op[1], op[2], op[3], op[4])

        nc.vector.memset(rows[:].bitcast(I32), 0)
        make_identity(nc, ident_b[:])
        make_identity(nc, ident_f[:])
        for i in range(2):
            nc.vector.memset(sel[i][:], 0.0)
            nc.vector.memset(sel[i][0:1, :], 1.0)
            nc.vector.memset(sel[i][32 * (i + 1):32 * (i + 1) + 1, :], 1.0)
        nc.vector.memset(warm[:], 0.0)
        nc.scalar.activation(out=warm[:], in_=warm[:], func=GELU)
        run(head, [], None)
        for us, ops in steps:
            res = o_pool.tile([P, len(us), NCOL], F32, name="res%d" % us[0], tag="res%d" % len(us),
                              bufs=(5 if len(us) < 4 else 3))
            for n in us:
                mx(n)
            run(ops, us, res)
